import numpy as np
import ml_dtypes


def mxq(x, axis, fmt="e4m3"):
    dtype, down = {"e4m3": (ml_dtypes.float8_e4m3fn, 7), "e5m2": (ml_dtypes.float8_e5m2, 14)}[fmt]
    v = np.moveaxis(np.asarray(x, np.float32).astype(ml_dtypes.bfloat16).astype(np.float64), axis, -1)
    blocks = v.reshape(v.shape[:-1] + (-1, 32))
    amax = np.abs(blocks).max(-1, keepdims=True)
    byte = np.maximum(np.where(amax > 0, np.frexp(amax)[1] - 1 + 127, 0) - down, 1)
    scale = np.exp2(byte - 127.0)
    codes = (blocks / scale).astype(np.float32).astype(dtype).astype(np.float64)
    return np.moveaxis((codes * scale).reshape(v.shape), -1, axis)


WIDE = False


def mx_kscale(k):
    if not WIDE:
        return np.ones(k)
    levels = np.array([10, -10, 5, -5, 0])
    a = np.random.permutation(np.resize(levels, k // 512 * 4)).reshape(k // 512, 4)
    idx = np.arange(k)
    return np.exp2(a[idx // 512, idx % 128 // 32])


BF16 = ml_dtypes.bfloat16


def bf(x):
    return np.asarray(x, np.float32).astype(BF16)


def f64(x):
    return np.asarray(x).astype(np.float64)


B, K, D, H1, H2, C = 256, 4, 2048, 1024, 512, 64
N = B * K


def setup_inputs():
    s = mx_kscale(D)
    return {"nf1": bf(np.random.standard_normal((N, D)) * s),
            "nf2": bf(np.random.standard_normal((N * K, D)) * s),
            "w1_0": bf(np.random.standard_normal((D, H1)) / np.sqrt(D) / s[:, None]),
            "w2_0": bf(np.random.standard_normal((D, H1)) / np.sqrt(D) / s[:, None])}


def sage_gcn(cur, neigh, w1, w2):
    b, d = cur.shape
    agg = neigh.reshape(b, -1, d).mean(axis=1)
    return np.maximum((mxq(cur, 1, "e4m3") @ mxq(w2, 0, "e4m3")) + (mxq(agg, 1, "e4m3") @ mxq(w1, 0, "e4m3")), 0.0)


def reference(nf1, nf2, w1_0, w2_0):
    return sage_gcn(f64(nf1), f64(nf2), f64(w1_0), f64(w2_0))

@@ -1,0 +1,222 @@
+from contextlib import ExitStack
+
+import concourse.mybir as mybir
+from concourse.masks import make_identity
+
+F32 = mybir.dt.float32
+BF16 = mybir.dt.bfloat16
+U32 = mybir.dt.uint32
+U8 = mybir.dt.uint8
+FP8X4 = mybir.dt.float8_e4m3fn_x4
+
+P = 128
+PACK = 4
+K_PASS = P * PACK
+PSUM_BANKS = 8
+N_TILE = 512
+
+NODES = 1024
+NEIGHBOURS = 4
+D = 2048
+H = 1024
+
+TILES = NODES // P
+PASSES = D // K_PASS
+CHUNKS = 2 * PASSES
+HALVES = H // N_TILE
+NODES_PER_ROWS = P // NEIGHBOURS
+WORDS_PER_PASS = K_PASS // 2
+PASSES_PER_BANK = 2
+
+FIRST = PSUM_BANKS // HALVES
+W_ROW_BUFFERS = 4
+
+FLOPS = 2 * 2 * NODES * D * H
+
+
+def tile_graphsage_pa_kernel(tc, nf1, nf2, w1_0, w2_0, out):
+    nc = tc.nc
+
+    own_view = nf1.rearrange("(m p) d -> m p d", p=P)
+    neigh_view = nf2.rearrange("(m q p) d -> m p q d", q=NEIGHBOURS, p=P)
+    out_view = out.rearrange("(m p) h -> m p h", p=P)
+    own_w_view = w2_0.rearrange("(g u p e) n -> g p u e n", u=2, p=P, e=2)
+    agg_w_view = w1_0.rearrange("(g t p) n -> g p t n", t=PACK, p=P)
+
+    with ExitStack() as ctx:
+        const = ctx.enter_context(tc.tile_pool(name="const", bufs=1))
+        keep = ctx.enter_context(tc.tile_pool(name="keep", bufs=1))
+        rows_pool = ctx.enter_context(tc.tile_pool(name="rows", bufs=FIRST))
+        grouped_pool = ctx.enter_context(tc.tile_pool(name="grouped", bufs=4))
+        banks = ctx.enter_context(tc.psum_pool(name="banks", bufs=PSUM_BANKS))
+        ctx.enter_context(tc.manual_schedule())
+
+        ident = const.tile([P, P], F32)
+        make_identity(nc, ident[:])
+        mean_f32 = const.tile([P, NODES_PER_ROWS], F32)
+        nc.vector.tensor_reduce(
+            out=mean_f32[:],
+            in_=ident[:].rearrange("p (i j) -> p i j", j=NEIGHBOURS),
+            axis=mybir.AxisListType.X,
+            op=mybir.AluOpType.add,
+        )
+        mean_cols = const.tile([P, NODES_PER_ROWS], BF16)
+        nc.vector.tensor_scalar_mul(out=mean_cols[:], in0=mean_f32[:], scalar1=1.0 / NEIGHBOURS)
+
+        w_codes = keep.tile([P, CHUNKS, H], U32, align_bytes=64)
+        w_scales = keep.tile([P, CHUNKS, H], U8, align_bytes=64)
+        x_codes = keep.tile([P, TILES, CHUNKS, P], U32, align_bytes=64)
+        x_scales = keep.tile([P, TILES, CHUNKS, P], U8, align_bytes=64)
+
+        own_rows, neigh_rows, acc = {}, {}, {}
+        w_rows, w_grouped = {}, {}
+
+        def load_node_tile(m):
+            own_rows[m] = rows_pool.tile([P, D], BF16, name="own_rows")
+            nc.sync.dma_start(out=own_rows[m][:], in_=own_view[m])
+            neigh_rows[m] = rows_pool.tile([P, NEIGHBOURS, D], BF16, name="neigh_rows")
+            nc.sync.dma_start(out=neigh_rows[m][:], in_=neigh_view[m])
+
+        def prepare_own(m):
+            row_words = own_rows[m][:].bitcast(F32)
+            own_grouped = {}
+            for first_pass in range(0, PASSES, PASSES_PER_BANK):
+                own_bank = banks.tile([P, PASSES_PER_BANK, 2, P], F32, tag="bank")
+                for i in range(PASSES_PER_BANK):
+                    for u in range(2):
+                        first_word = (first_pass + i) * WORDS_PER_PASS + u * P
+                        nc.tensor.transpose(
+                            own_bank[:, i, u, :], row_words[:, first_word : first_word + P], ident[:]
+                        )
+                own_grouped[first_pass] = grouped_pool.tile(
+                    [P, PASSES_PER_BANK * P * PACK], BF16, name="own_grouped", align_bytes=64
+                )
+                nc.vector.tensor_copy(
+                    out=own_grouped[first_pass][:]
+                    .bitcast(F32)
+                    .rearrange("p (g r u) -> p g r u", g=PASSES_PER_BANK, u=2),
+                    in_=own_bank[:].rearrange("p g u r -> p g r u"),
+                )
+            for first_pass in range(0, PASSES, PASSES_PER_BANK):
+                chunks = slice(first_pass, first_pass + PASSES_PER_BANK)
+                nc.vector.quantize_mx(
+                    out=x_codes[:, m, chunks, :].rearrange("p c r -> p (c r)").bitcast(FP8X4),
+                    scales=x_scales[:, m, chunks, :].rearrange("p c r -> p (c r)"),
+                    in_=own_grouped[first_pass][:],
+                )
+
+        def prepare_agg(m, g):
+            agg_bank = banks.tile([P, PACK, P], F32, tag="bank")
+            for q in range(NEIGHBOURS):
+                nodes = slice(q * NODES_PER_ROWS, (q + 1) * NODES_PER_ROWS)
+                for t in range(PACK):
+                    first_d = g * K_PASS + t * P
+                    nc.tensor.matmul(
+                        out=agg_bank[:, t, nodes],
+                        lhsT=neigh_rows[m][:, q, first_d : first_d + P],
+                        rhs=mean_cols[:],
+                        start=True,
+                        stop=True,
+                    )
+            agg_grouped = grouped_pool.tile([P, P, PACK], BF16, align_bytes=64)
+            nc.scalar.copy(out=agg_grouped[:], in_=agg_bank[:].rearrange("p t r -> p r t"))
+            nc.vector.quantize_mx(
+                out=x_codes[:, m, PASSES + g, :].bitcast(FP8X4),
+                scales=x_scales[:, m, PASSES + g, :],
+                in_=agg_grouped[:].rearrange("p r t -> p (r t)"),
+            )
+
+        def prepare(m):
+            prepare_own(m)
+            for g in range(PASSES):
+                prepare_agg(m, g)
+
+        def multiply(m, c):
+            if c == 0:
+                acc[m] = [
+                    banks.tile([P, N_TILE], F32, name="acc", tag="bank") for half in range(HALVES)
+                ]
+            for half in range(HALVES):
+                cols = slice(half * N_TILE, (half + 1) * N_TILE)
+                nc.tensor.matmul_mx(
+                    out=acc[m][half][:],
+                    lhsT=x_codes[:, m, c, :].bitcast(FP8X4),
+                    lhsT_scale=x_scales[:, m, c, :],
+                    rhs=w_codes[:, c, cols].bitcast(FP8X4),
+                    rhs_scale=w_scales[:, c, cols],
+                    start=(c == 0),
+                    stop=(c == CHUNKS - 1),
+                )
+
+        for m in range(FIRST):
+            load_node_tile(m)
+
+        with ExitStack() as weights_ctx:
+            w_rows_pool = weights_ctx.enter_context(
+                tc.tile_pool(name="w_rows", bufs=W_ROW_BUFFERS)
+            )
+            w_grouped_pool = weights_ctx.enter_context(tc.tile_pool(name="w_grouped", bufs=3))
+
+            def load_weight_chunk(c):
+                w_rows[c] = w_rows_pool.tile([P, PACK, H], BF16, name="w_rows")
+                if c < PASSES:
+                    nc.sync.dma_start(
+                        out=w_rows[c][:].rearrange("p (u e) n -> p u e n", e=2), in_=own_w_view[c]
+                    )
+                else:
+                    nc.sync.dma_start(out=w_rows[c][:], in_=agg_w_view[c - PASSES])
+
+            def regroup_weight_chunk(c):
+                w_grouped[c] = w_grouped_pool.tile(
+                    [P, H, PACK], BF16, name="w_grouped", align_bytes=64
+                )
+                grouped = w_grouped[c][:].rearrange("p (a i) t -> p a t i", i=4)
+                rows = w_rows[c][:].rearrange("p t (a i) -> p a t i", i=4)
+                middle = H // 4 // 2
+                nc.vector.tensor_copy(out=grouped[:, :middle], in_=rows[:, :middle])
+                nc.scalar.copy(out=grouped[:, middle:], in_=rows[:, middle:])
+
+            def quantise_weight_chunk(c):
+                nc.vector.quantize_mx(
+                    out=w_codes[:, c, :].bitcast(FP8X4),
+                    scales=w_scales[:, c, :],
+                    in_=w_grouped[c][:].rearrange("p n t -> p (n t)"),
+                )
+
+            for c in range(W_ROW_BUFFERS):
+                load_weight_chunk(c)
+
+            for m in range(FIRST):
+                prepare(m)
+
+            regroup_weight_chunk(0)
+            for c in range(CHUNKS):
+                if c + 1 < CHUNKS:
+                    regroup_weight_chunk(c + 1)
+                quantise_weight_chunk(c)
+                if c + W_ROW_BUFFERS < CHUNKS:
+                    load_weight_chunk(c + W_ROW_BUFFERS)
+                for m in range(FIRST):
+                    multiply(m, c)
+
+        for m in range(FIRST, TILES):
+            load_node_tile(m)
+
+        result_pool = ctx.enter_context(tc.tile_pool(name="result", bufs=TILES))
+
+        def finish(m):
+            result = result_pool.tile([P, H], F32)
+            nc.vector.tensor_scalar_max(out=result[:, 0:N_TILE], in0=acc[m][0][:], scalar1=0.0)
+            nc.scalar.activation(
+                out=result[:, N_TILE:H], in_=acc[m][1][:], func=mybir.ActivationFunctionType.Relu
+            )
+            nc.sync.dma_start(out=out_view[m], in_=result[:])
+
+        for m in range(FIRST):
+            finish(m)
+
+        for m in range(FIRST, TILES):
+            prepare(m)
+            for c in range(CHUNKS):
+                multiply(m, c)
+            finish(m)

@@ -22,6 +22,7 @@ H = 1024
 
 TILES = NODES // P
 PASSES = D // K_PASS
+OWN, AGG = 0, 1
 CHUNKS = 2 * PASSES
 HALVES = H // N_TILE
 NODES_PER_ROWS = P // NEIGHBOURS
@@ -29,6 +30,8 @@ WORDS_PER_PASS = K_PASS // 2
 PASSES_PER_BANK = 2
 
 FIRST = PSUM_BANKS // HALVES
+OWN_ROW_BUFFERS = 4
+NEIGH_ROW_BUFFERS = 3
 W_ROW_BUFFERS = 4
 
 FLOPS = 2 * 2 * NODES * D * H
@@ -46,8 +49,15 @@ def tile_graphsage_pa_kernel(tc, nf1, nf2, w1_0, w2_0, out):
     with ExitStack() as ctx:
         const = ctx.enter_context(tc.tile_pool(name="const", bufs=1))
         keep = ctx.enter_context(tc.tile_pool(name="keep", bufs=1))
-        rows_pool = ctx.enter_context(tc.tile_pool(name="rows", bufs=FIRST))
-        grouped_pool = ctx.enter_context(tc.tile_pool(name="grouped", bufs=4))
+        own_rows_pool = ctx.enter_context(tc.tile_pool(name="own_rows", bufs=OWN_ROW_BUFFERS))
+        neigh_rows_pool = ctx.enter_context(
+            tc.tile_pool(name="neigh_rows", bufs=NEIGH_ROW_BUFFERS)
+        )
+        w_rows_pool = ctx.enter_context(tc.tile_pool(name="w_rows", bufs=W_ROW_BUFFERS))
+        w_grouped_pool = ctx.enter_context(tc.tile_pool(name="w_grouped", bufs=3))
+        own_grouped_pool = ctx.enter_context(tc.tile_pool(name="own_grouped", bufs=2))
+        agg_grouped_pool = ctx.enter_context(tc.tile_pool(name="agg_grouped", bufs=4))
+        agg_mx_pool = ctx.enter_context(tc.tile_pool(name="agg_mx", bufs=2))
         banks = ctx.enter_context(tc.psum_pool(name="banks", bufs=PSUM_BANKS))
         ctx.enter_context(tc.manual_schedule())
 
@@ -65,21 +75,55 @@ def tile_graphsage_pa_kernel(tc, nf1, nf2, w1_0, w2_0, out):
 
         w_codes = keep.tile([P, CHUNKS, H], U32, align_bytes=64)
         w_scales = keep.tile([P, CHUNKS, H], U8, align_bytes=64)
-        x_codes = keep.tile([P, TILES, CHUNKS, P], U32, align_bytes=64)
-        x_scales = keep.tile([P, TILES, CHUNKS, P], U8, align_bytes=64)
+        own_codes = keep.tile([P, TILES, PASSES, P], U32, align_bytes=64)
+        own_scales = keep.tile([P, TILES, PASSES, P], U8, align_bytes=64)
+        result = keep.tile([P, TILES, H], F32)
 
-        own_rows, neigh_rows, acc = {}, {}, {}
-        w_rows, w_grouped = {}, {}
+        own_rows, neigh_rows, w_rows, w_grouped = {}, {}, {}, {}
+        x_codes, x_scales, acc = {}, {}, {}
 
-        def load_node_tile(m):
-            own_rows[m] = rows_pool.tile([P, D], BF16, name="own_rows")
+        def load_own_rows(m):
+            own_rows[m] = own_rows_pool.tile([P, D], BF16, name="own_rows")
             nc.sync.dma_start(out=own_rows[m][:], in_=own_view[m])
-            neigh_rows[m] = rows_pool.tile([P, NEIGHBOURS, D], BF16, name="neigh_rows")
+
+        def load_neigh_rows(m):
+            neigh_rows[m] = neigh_rows_pool.tile([P, NEIGHBOURS, D], BF16, name="neigh_rows")
             nc.sync.dma_start(out=neigh_rows[m][:], in_=neigh_view[m])
+
+        def load_weight_chunk(c):
+            w_rows[c] = w_rows_pool.tile([P, PACK, H], BF16, name="w_rows")
+            if c < PASSES:
+                nc.sync.dma_start(
+                    out=w_rows[c][:].rearrange("p (u e) n -> p u e n", e=2), in_=own_w_view[c]
+                )
+            else:
+                nc.sync.dma_start(out=w_rows[c][:], in_=agg_w_view[c - PASSES])
+
+        def regroup_weight_chunk(c):
+            w_grouped[c] = w_grouped_pool.tile([P, H, PACK], BF16, name="w_grouped", align_bytes=64)
+            grouped = w_grouped[c][:].rearrange("p (a i) t -> p a t i", i=4)
+            rows = w_rows[c][:].rearrange("p t (a i) -> p a t i", i=4)
+            middle = H // 4 // 2
+            nc.vector.tensor_copy(out=grouped[:, :middle], in_=rows[:, :middle])
+            nc.scalar.copy(out=grouped[:, middle:], in_=rows[:, middle:])
+
+        def quantise_weight_chunk(c):
+            if c + 1 < CHUNKS:
+                regroup_weight_chunk(c + 1)
+            nc.vector.quantize_mx(
+                out=w_codes[:, c, :].bitcast(FP8X4),
+                scales=w_scales[:, c, :],
+                in_=w_grouped[c][:].rearrange("p n t -> p (n t)"),
+            )
+            if c + W_ROW_BUFFERS < CHUNKS:
+                load_weight_chunk(c + W_ROW_BUFFERS)
 
         def prepare_own(m):
             row_words = own_rows[m][:].bitcast(F32)
-            own_grouped = {}
+            own_grouped = own_grouped_pool.tile([P, PASSES * P * PACK], BF16, align_bytes=64)
+            grouped_words = own_grouped[:].bitcast(F32).rearrange(
+                "p (g r u) -> p g r u", g=PASSES, u=2
+            )
             for first_pass in range(0, PASSES, PASSES_PER_BANK):
                 own_bank = banks.tile([P, PASSES_PER_BANK, 2, P], F32, tag="bank")
                 for i in range(PASSES_PER_BANK):
@@ -88,135 +132,106 @@ def tile_graphsage_pa_kernel(tc, nf1, nf2, w1_0, w2_0, out):
                         nc.tensor.transpose(
                             own_bank[:, i, u, :], row_words[:, first_word : first_word + P], ident[:]
                         )
-                own_grouped[first_pass] = grouped_pool.tile(
-                    [P, PASSES_PER_BANK * P * PACK], BF16, name="own_grouped", align_bytes=64
-                )
-                nc.vector.tensor_copy(
-                    out=own_grouped[first_pass][:]
-                    .bitcast(F32)
-                    .rearrange("p (g r u) -> p g r u", g=PASSES_PER_BANK, u=2),
+                nc.scalar.copy(
+                    out=grouped_words[:, first_pass : first_pass + PASSES_PER_BANK],
                     in_=own_bank[:].rearrange("p g u r -> p g r u"),
                 )
-            for first_pass in range(0, PASSES, PASSES_PER_BANK):
-                chunks = slice(first_pass, first_pass + PASSES_PER_BANK)
-                nc.vector.quantize_mx(
-                    out=x_codes[:, m, chunks, :].rearrange("p c r -> p (c r)").bitcast(FP8X4),
-                    scales=x_scales[:, m, chunks, :].rearrange("p c r -> p (c r)"),
-                    in_=own_grouped[first_pass][:],
-                )
-
-        def prepare_agg(m, g):
-            agg_bank = banks.tile([P, PACK, P], F32, tag="bank")
-            for q in range(NEIGHBOURS):
-                nodes = slice(q * NODES_PER_ROWS, (q + 1) * NODES_PER_ROWS)
-                for t in range(PACK):
-                    first_d = g * K_PASS + t * P
-                    nc.tensor.matmul(
-                        out=agg_bank[:, t, nodes],
-                        lhsT=neigh_rows[m][:, q, first_d : first_d + P],
-                        rhs=mean_cols[:],
-                        start=True,
-                        stop=True,
-                    )
-            agg_grouped = grouped_pool.tile([P, P, PACK], BF16, align_bytes=64)
-            nc.scalar.copy(out=agg_grouped[:], in_=agg_bank[:].rearrange("p t r -> p r t"))
+            x_codes[m, OWN] = own_codes[:, m]
+            x_scales[m, OWN] = own_scales[:, m]
             nc.vector.quantize_mx(
-                out=x_codes[:, m, PASSES + g, :].bitcast(FP8X4),
-                scales=x_scales[:, m, PASSES + g, :],
-                in_=agg_grouped[:].rearrange("p r t -> p (r t)"),
+                out=x_codes[m, OWN].rearrange("p g r -> p (g r)").bitcast(FP8X4),
+                scales=x_scales[m, OWN].rearrange("p g r -> p (g r)"),
+                in_=own_grouped[:],
             )
 
-        def prepare(m):
-            prepare_own(m)
+        def prepare_agg(m):
+            agg_codes = agg_mx_pool.tile([P, PASSES, P], U32, align_bytes=64)
+            agg_scales = agg_mx_pool.tile([P, PASSES, P], U8, align_bytes=64)
+            x_codes[m, AGG] = agg_codes[:]
+            x_scales[m, AGG] = agg_scales[:]
             for g in range(PASSES):
-                prepare_agg(m, g)
+                agg_bank = banks.tile([P, PACK, P], F32, tag="bank")
+                for q in range(NEIGHBOURS):
+                    nodes = slice(q * NODES_PER_ROWS, (q + 1) * NODES_PER_ROWS)
+                    for t in range(PACK):
+                        first_d = g * K_PASS + t * P
+                        nc.tensor.matmul(
+                            out=agg_bank[:, t, nodes],
+                            lhsT=neigh_rows[m][:, q, first_d : first_d + P],
+                            rhs=mean_cols[:],
+                            start=True,
+                            stop=True,
+                        )
+                agg_grouped = agg_grouped_pool.tile([P, P, PACK], BF16, align_bytes=64)
+                nc.scalar.copy(out=agg_grouped[:], in_=agg_bank[:].rearrange("p t r -> p r t"))
+                nc.vector.quantize_mx(
+                    out=agg_codes[:, g, :].bitcast(FP8X4),
+                    scales=agg_scales[:, g, :],
+                    in_=agg_grouped[:].rearrange("p r t -> p (r t)"),
+                )
 
-        def multiply(m, c):
-            if c == 0:
-                acc[m] = [
+        def multiply(m, product, g):
+            if g == 0:
+                acc[m, product] = [
                     banks.tile([P, N_TILE], F32, name="acc", tag="bank") for half in range(HALVES)
                 ]
+            c = PASSES * product + g
             for half in range(HALVES):
                 cols = slice(half * N_TILE, (half + 1) * N_TILE)
                 nc.tensor.matmul_mx(
-                    out=acc[m][half][:],
-                    lhsT=x_codes[:, m, c, :].bitcast(FP8X4),
-                    lhsT_scale=x_scales[:, m, c, :],
+                    out=acc[m, product][half][:],
+                    lhsT=x_codes[m, product][:, g, :].bitcast(FP8X4),
+                    lhsT_scale=x_scales[m, product][:, g, :],
                     rhs=w_codes[:, c, cols].bitcast(FP8X4),
                     rhs_scale=w_scales[:, c, cols],
-                    start=(c == 0),
-                    stop=(c == CHUNKS - 1),
+                    start=(g == 0),
+                    stop=(g == PASSES - 1),
                 )
 
-        for m in range(FIRST):
-            load_node_tile(m)
-
-        with ExitStack() as weights_ctx:
-            w_rows_pool = weights_ctx.enter_context(
-                tc.tile_pool(name="w_rows", bufs=W_ROW_BUFFERS)
-            )
-            w_grouped_pool = weights_ctx.enter_context(tc.tile_pool(name="w_grouped", bufs=3))
-
-            def load_weight_chunk(c):
-                w_rows[c] = w_rows_pool.tile([P, PACK, H], BF16, name="w_rows")
-                if c < PASSES:
-                    nc.sync.dma_start(
-                        out=w_rows[c][:].rearrange("p (u e) n -> p u e n", e=2), in_=own_w_view[c]
-                    )
-                else:
-                    nc.sync.dma_start(out=w_rows[c][:], in_=agg_w_view[c - PASSES])
-
-            def regroup_weight_chunk(c):
-                w_grouped[c] = w_grouped_pool.tile(
-                    [P, H, PACK], BF16, name="w_grouped", align_bytes=64
-                )
-                grouped = w_grouped[c][:].rearrange("p (a i) t -> p a t i", i=4)
-                rows = w_rows[c][:].rearrange("p t (a i) -> p a t i", i=4)
-                middle = H // 4 // 2
-                nc.vector.tensor_copy(out=grouped[:, :middle], in_=rows[:, :middle])
-                nc.scalar.copy(out=grouped[:, middle:], in_=rows[:, middle:])
-
-            def quantise_weight_chunk(c):
-                nc.vector.quantize_mx(
-                    out=w_codes[:, c, :].bitcast(FP8X4),
-                    scales=w_scales[:, c, :],
-                    in_=w_grouped[c][:].rearrange("p n t -> p (n t)"),
-                )
-
-            for c in range(W_ROW_BUFFERS):
-                load_weight_chunk(c)
-
-            for m in range(FIRST):
-                prepare(m)
-
-            regroup_weight_chunk(0)
-            for c in range(CHUNKS):
-                if c + 1 < CHUNKS:
-                    regroup_weight_chunk(c + 1)
-                quantise_weight_chunk(c)
-                if c + W_ROW_BUFFERS < CHUNKS:
-                    load_weight_chunk(c + W_ROW_BUFFERS)
-                for m in range(FIRST):
-                    multiply(m, c)
-
-        for m in range(FIRST, TILES):
-            load_node_tile(m)
-
-        result_pool = ctx.enter_context(tc.tile_pool(name="result", bufs=TILES))
+        def set_aside(m):
+            nc.vector.tensor_copy(out=result[:, m, 0:N_TILE], in_=acc[m, OWN][0][:])
+            nc.scalar.copy(out=result[:, m, N_TILE:H], in_=acc[m, OWN][1][:])
 
         def finish(m):
-            result = result_pool.tile([P, H], F32)
-            nc.vector.tensor_scalar_max(out=result[:, 0:N_TILE], in0=acc[m][0][:], scalar1=0.0)
-            nc.scalar.activation(
-                out=result[:, N_TILE:H], in_=acc[m][1][:], func=mybir.ActivationFunctionType.Relu
-            )
-            nc.sync.dma_start(out=out_view[m], in_=result[:])
+            for half in range(HALVES):
+                cols = slice(half * N_TILE, (half + 1) * N_TILE)
+                nc.vector.tensor_add(
+                    out=result[:, m, cols], in0=acc[m, AGG][half][:], in1=result[:, m, cols]
+                )
+            nc.vector.tensor_scalar_max(out=result[:, m, :], in0=result[:, m, :], scalar1=0.0)
 
+        for m in range(OWN_ROW_BUFFERS):
+            load_own_rows(m)
+        for m in range(TILES):
+            prepare_own(m)
+            if m + OWN_ROW_BUFFERS < TILES:
+                load_own_rows(m + OWN_ROW_BUFFERS)
+
+        for c in range(W_ROW_BUFFERS):
+            load_weight_chunk(c)
+        regroup_weight_chunk(0)
+        for g in range(PASSES):
+            quantise_weight_chunk(PASSES * OWN + g)
+            for m in range(FIRST):
+                multiply(m, OWN, g)
         for m in range(FIRST):
+            set_aside(m)
+        for g in range(PASSES):
+            quantise_weight_chunk(PASSES * AGG + g)
+        for m in range(FIRST, TILES):
+            for g in range(PASSES):
+                multiply(m, OWN, g)
+            set_aside(m)
+
+        for m in range(NEIGH_ROW_BUFFERS):
+            load_neigh_rows(m)
+        for m in range(TILES):
+            prepare_agg(m)
+            if m + NEIGH_ROW_BUFFERS < TILES:
+                load_neigh_rows(m + NEIGH_ROW_BUFFERS)
+            for g in range(PASSES):
+                multiply(m, AGG, g)
             finish(m)
 
-        for m in range(FIRST, TILES):
-            prepare(m)
-            for c in range(CHUNKS):
-                multiply(m, c)
-            finish(m)
+        for m in range(TILES):
+            nc.sync.dma_start(out=out_view[m], in_=result[:, m, :])

@@ -30,8 +30,7 @@ WORDS_PER_PASS = K_PASS // 2
 PASSES_PER_BANK = 2
 
 FIRST = PSUM_BANKS // HALVES
-OWN_ROW_BUFFERS = 4
-NEIGH_ROW_BUFFERS = 3
+ROW_BUFFERS = 4
 W_ROW_BUFFERS = 4
 
 FLOPS = 2 * 2 * NODES * D * H
@@ -49,10 +48,7 @@ def tile_graphsage_pa_kernel(tc, nf1, nf2, w1_0, w2_0, out):
     with ExitStack() as ctx:
         const = ctx.enter_context(tc.tile_pool(name="const", bufs=1))
         keep = ctx.enter_context(tc.tile_pool(name="keep", bufs=1))
-        own_rows_pool = ctx.enter_context(tc.tile_pool(name="own_rows", bufs=OWN_ROW_BUFFERS))
-        neigh_rows_pool = ctx.enter_context(
-            tc.tile_pool(name="neigh_rows", bufs=NEIGH_ROW_BUFFERS)
-        )
+        rows_pool = ctx.enter_context(tc.tile_pool(name="rows", bufs=ROW_BUFFERS))
         w_rows_pool = ctx.enter_context(tc.tile_pool(name="w_rows", bufs=W_ROW_BUFFERS))
         w_grouped_pool = ctx.enter_context(tc.tile_pool(name="w_grouped", bufs=3))
         own_grouped_pool = ctx.enter_context(tc.tile_pool(name="own_grouped", bufs=2))
@@ -82,13 +78,16 @@ def tile_graphsage_pa_kernel(tc, nf1, nf2, w1_0, w2_0, out):
         own_rows, neigh_rows, w_rows, w_grouped = {}, {}, {}, {}
         x_codes, x_scales, acc = {}, {}, {}
 
-        def load_own_rows(m):
-            own_rows[m] = own_rows_pool.tile([P, D], BF16, name="own_rows")
-            nc.sync.dma_start(out=own_rows[m][:], in_=own_view[m])
+        def load_own_rows(first_tile):
+            row_buffer = rows_pool.tile([P, NEIGHBOURS, D], BF16)
+            for j in range(NEIGHBOURS):
+                own_rows[first_tile + j] = row_buffer[:, j, :]
+                nc.sync.dma_start(out=row_buffer[:, j, :], in_=own_view[first_tile + j])
 
         def load_neigh_rows(m):
-            neigh_rows[m] = neigh_rows_pool.tile([P, NEIGHBOURS, D], BF16, name="neigh_rows")
-            nc.sync.dma_start(out=neigh_rows[m][:], in_=neigh_view[m])
+            row_buffer = rows_pool.tile([P, NEIGHBOURS, D], BF16)
+            neigh_rows[m] = row_buffer
+            nc.sync.dma_start(out=row_buffer[:], in_=neigh_view[m])
 
         def load_weight_chunk(c):
             w_rows[c] = w_rows_pool.tile([P, PACK, H], BF16, name="w_rows")
@@ -119,7 +118,7 @@ def tile_graphsage_pa_kernel(tc, nf1, nf2, w1_0, w2_0, out):
                 load_weight_chunk(c + W_ROW_BUFFERS)
 
         def prepare_own(m):
-            row_words = own_rows[m][:].bitcast(F32)
+            row_words = own_rows[m].bitcast(F32)
             own_grouped = own_grouped_pool.tile([P, PASSES * P * PACK], BF16, align_bytes=64)
             grouped_words = own_grouped[:].bitcast(F32).rearrange(
                 "p (g r u) -> p g r u", g=PASSES, u=2
@@ -144,31 +143,31 @@ def tile_graphsage_pa_kernel(tc, nf1, nf2, w1_0, w2_0, out):
                 in_=own_grouped[:],
             )
 
-        def prepare_agg(m):
-            agg_codes = agg_mx_pool.tile([P, PASSES, P], U32, align_bytes=64)
-            agg_scales = agg_mx_pool.tile([P, PASSES, P], U8, align_bytes=64)
-            x_codes[m, AGG] = agg_codes[:]
-            x_scales[m, AGG] = agg_scales[:]
-            for g in range(PASSES):
-                agg_bank = banks.tile([P, PACK, P], F32, tag="bank")
-                for q in range(NEIGHBOURS):
-                    nodes = slice(q * NODES_PER_ROWS, (q + 1) * NODES_PER_ROWS)
-                    for t in range(PACK):
-                        first_d = g * K_PASS + t * P
-                        nc.tensor.matmul(
-                            out=agg_bank[:, t, nodes],
-                            lhsT=neigh_rows[m][:, q, first_d : first_d + P],
-                            rhs=mean_cols[:],
-                            start=True,
-                            stop=True,
-                        )
-                agg_grouped = agg_grouped_pool.tile([P, P, PACK], BF16, align_bytes=64)
-                nc.scalar.copy(out=agg_grouped[:], in_=agg_bank[:].rearrange("p t r -> p r t"))
-                nc.vector.quantize_mx(
-                    out=agg_codes[:, g, :].bitcast(FP8X4),
-                    scales=agg_scales[:, g, :],
-                    in_=agg_grouped[:].rearrange("p r t -> p (r t)"),
-                )
+        def prepare_agg(m, g):
+            if g == 0:
+                agg_codes = agg_mx_pool.tile([P, PASSES, P], U32, align_bytes=64)
+                agg_scales = agg_mx_pool.tile([P, PASSES, P], U8, align_bytes=64)
+                x_codes[m, AGG] = agg_codes[:]
+                x_scales[m, AGG] = agg_scales[:]
+            agg_bank = banks.tile([P, PACK, P], F32, tag="bank")
+            for q in range(NEIGHBOURS):
+                nodes = slice(q * NODES_PER_ROWS, (q + 1) * NODES_PER_ROWS)
+                for t in range(PACK):
+                    first_d = g * K_PASS + t * P
+                    nc.tensor.matmul(
+                        out=agg_bank[:, t, nodes],
+                        lhsT=neigh_rows[m][:, q, first_d : first_d + P],
+                        rhs=mean_cols[:],
+                        start=True,
+                        stop=True,
+                    )
+            agg_grouped = agg_grouped_pool.tile([P, P, PACK], BF16, align_bytes=64)
+            nc.scalar.copy(out=agg_grouped[:], in_=agg_bank[:].rearrange("p t r -> p r t"))
+            nc.vector.quantize_mx(
+                out=x_codes[m, AGG][:, g, :].bitcast(FP8X4),
+                scales=x_scales[m, AGG][:, g, :],
+                in_=agg_grouped[:].rearrange("p r t -> p (r t)"),
+            )
 
         def multiply(m, product, g):
             if g == 0:
@@ -200,12 +199,10 @@ def tile_graphsage_pa_kernel(tc, nf1, nf2, w1_0, w2_0, out):
                 )
             nc.vector.tensor_scalar_max(out=result[:, m, :], in0=result[:, m, :], scalar1=0.0)
 
-        for m in range(OWN_ROW_BUFFERS):
-            load_own_rows(m)
+        for first_tile in range(0, TILES, NEIGHBOURS):
+            load_own_rows(first_tile)
         for m in range(TILES):
             prepare_own(m)
-            if m + OWN_ROW_BUFFERS < TILES:
-                load_own_rows(m + OWN_ROW_BUFFERS)
 
         for c in range(W_ROW_BUFFERS):
             load_weight_chunk(c)
@@ -223,14 +220,17 @@ def tile_graphsage_pa_kernel(tc, nf1, nf2, w1_0, w2_0, out):
                 multiply(m, OWN, g)
             set_aside(m)
 
-        for m in range(NEIGH_ROW_BUFFERS):
+        for m in range(ROW_BUFFERS):
             load_neigh_rows(m)
+        for g in range(PASSES):
+            prepare_agg(0, g)
         for m in range(TILES):
-            prepare_agg(m)
-            if m + NEIGH_ROW_BUFFERS < TILES:
-                load_neigh_rows(m + NEIGH_ROW_BUFFERS)
+            if m + ROW_BUFFERS < TILES:
+                load_neigh_rows(m + ROW_BUFFERS)
             for g in range(PASSES):
                 multiply(m, AGG, g)
+                if m + 1 < TILES:
+                    prepare_agg(m + 1, g)
             finish(m)
 
         for m in range(TILES):

@@ -222,16 +222,16 @@ def tile_graphsage_pa_kernel(tc, nf1, nf2, w1_0, w2_0, out):
 
         for m in range(ROW_BUFFERS):
             load_neigh_rows(m)
-        for g in range(PASSES):
-            prepare_agg(0, g)
         for m in range(TILES):
+            for g in range(PASSES):
+                prepare_agg(m, g)
             if m + ROW_BUFFERS < TILES:
                 load_neigh_rows(m + ROW_BUFFERS)
+            if m > 0:
+                finish(m - 1)
             for g in range(PASSES):
                 multiply(m, AGG, g)
-                if m + 1 < TILES:
-                    prepare_agg(m + 1, g)
-            finish(m)
+        finish(TILES - 1)
 
         for m in range(TILES):
             nc.sync.dma_start(out=out_view[m], in_=result[:, m, :])

from contextlib import ExitStack

import concourse.mybir as mybir
from concourse.masks import make_identity

F32 = mybir.dt.float32
BF16 = mybir.dt.bfloat16
U32 = mybir.dt.uint32
U8 = mybir.dt.uint8
FP8X4 = mybir.dt.float8_e4m3fn_x4

P = 128
PACK = 4
K_PASS = P * PACK
PSUM_BANKS = 8
N_TILE = 512

NODES = 1024
NEIGHBOURS = 4
D = 2048
H = 1024

TILES = NODES // P
PASSES = D // K_PASS
OWN, AGG = 0, 1
CHUNKS = 2 * PASSES
HALVES = H // N_TILE
NODES_PER_ROWS = P // NEIGHBOURS
WORDS_PER_PASS = K_PASS // 2
PASSES_PER_BANK = 2

FIRST = PSUM_BANKS // HALVES
ROW_BUFFERS = 4
W_ROW_BUFFERS = 4

FLOPS = 2 * 2 * NODES * D * H


def tile_graphsage_pa_kernel(tc, nf1, nf2, w1_0, w2_0, out):
    nc = tc.nc

    own_view = nf1.rearrange("(m p) d -> m p d", p=P)
    neigh_view = nf2.rearrange("(m q p) d -> m p q d", q=NEIGHBOURS, p=P)
    out_view = out.rearrange("(m p) h -> m p h", p=P)
    own_w_view = w2_0.rearrange("(g u p e) n -> g p u e n", u=2, p=P, e=2)
    agg_w_view = w1_0.rearrange("(g t p) n -> g p t n", t=PACK, p=P)

    with ExitStack() as ctx:
        const = ctx.enter_context(tc.tile_pool(name="const", bufs=1))
        keep = ctx.enter_context(tc.tile_pool(name="keep", bufs=1))
        rows_pool = ctx.enter_context(tc.tile_pool(name="rows", bufs=ROW_BUFFERS))
        w_rows_pool = ctx.enter_context(tc.tile_pool(name="w_rows", bufs=W_ROW_BUFFERS))
        w_grouped_pool = ctx.enter_context(tc.tile_pool(name="w_grouped", bufs=3))
        own_grouped_pool = ctx.enter_context(tc.tile_pool(name="own_grouped", bufs=2))
        agg_grouped_pool = ctx.enter_context(tc.tile_pool(name="agg_grouped", bufs=4))
        agg_mx_pool = ctx.enter_context(tc.tile_pool(name="agg_mx", bufs=2))
        banks = ctx.enter_context(tc.psum_pool(name="banks", bufs=PSUM_BANKS))
        ctx.enter_context(tc.manual_schedule())

        ident = const.tile([P, P], F32)
        make_identity(nc, ident[:])
        mean_f32 = const.tile([P, NODES_PER_ROWS], F32)
        nc.vector.tensor_reduce(
            out=mean_f32[:],
            in_=ident[:].rearrange("p (i j) -> p i j", j=NEIGHBOURS),
            axis=mybir.AxisListType.X,
            op=mybir.AluOpType.add,
        )
        mean_cols = const.tile([P, NODES_PER_ROWS], BF16)
        nc.vector.tensor_scalar_mul(out=mean_cols[:], in0=mean_f32[:], scalar1=1.0 / NEIGHBOURS)

        w_codes = keep.tile([P, CHUNKS, H], U32, align_bytes=64)
        w_scales = keep.tile([P, CHUNKS, H], U8, align_bytes=64)
        own_codes = keep.tile([P, TILES, PASSES, P], U32, align_bytes=64)
        own_scales = keep.tile([P, TILES, PASSES, P], U8, align_bytes=64)
        result = keep.tile([P, TILES, H], F32)

        own_rows, neigh_rows, w_rows, w_grouped = {}, {}, {}, {}
        x_codes, x_scales, acc = {}, {}, {}

        def load_own_rows(first_tile):
            row_buffer = rows_pool.tile([P, NEIGHBOURS, D], BF16)
            for j in range(NEIGHBOURS):
                own_rows[first_tile + j] = row_buffer[:, j, :]
                nc.sync.dma_start(out=row_buffer[:, j, :], in_=own_view[first_tile + j])

        def load_neigh_rows(m):
            row_buffer = rows_pool.tile([P, NEIGHBOURS, D], BF16)
            neigh_rows[m] = row_buffer
            nc.sync.dma_start(out=row_buffer[:], in_=neigh_view[m])

        def load_weight_chunk(c):
            w_rows[c] = w_rows_pool.tile([P, PACK, H], BF16, name="w_rows")
            if c < PASSES:
                nc.sync.dma_start(
                    out=w_rows[c][:].rearrange("p (u e) n -> p u e n", e=2), in_=own_w_view[c]
                )
            else:
                nc.sync.dma_start(out=w_rows[c][:], in_=agg_w_view[c - PASSES])

        def regroup_weight_chunk(c):
            w_grouped[c] = w_grouped_pool.tile([P, H, PACK], BF16, name="w_grouped", align_bytes=64)
            grouped = w_grouped[c][:].rearrange("p (a i) t -> p a t i", i=4)
            rows = w_rows[c][:].rearrange("p t (a i) -> p a t i", i=4)
            middle = H // 4 // 2
            nc.vector.tensor_copy(out=grouped[:, :middle], in_=rows[:, :middle])
            nc.scalar.copy(out=grouped[:, middle:], in_=rows[:, middle:])

        def quantise_weight_chunk(c):
            if c + 1 < CHUNKS:
                regroup_weight_chunk(c + 1)
            nc.vector.quantize_mx(
                out=w_codes[:, c, :].bitcast(FP8X4),
                scales=w_scales[:, c, :],
                in_=w_grouped[c][:].rearrange("p n t -> p (n t)"),
            )
            if c + W_ROW_BUFFERS < CHUNKS:
                load_weight_chunk(c + W_ROW_BUFFERS)

        def prepare_own(m):
            row_words = own_rows[m].bitcast(F32)
            own_grouped = own_grouped_pool.tile([P, PASSES * P * PACK], BF16, align_bytes=64)
            grouped_words = own_grouped[:].bitcast(F32).rearrange(
                "p (g r u) -> p g r u", g=PASSES, u=2
            )
            for first_pass in range(0, PASSES, PASSES_PER_BANK):
                own_bank = banks.tile([P, PASSES_PER_BANK, 2, P], F32, tag="bank")
                for i in range(PASSES_PER_BANK):
                    for u in range(2):
                        first_word = (first_pass + i) * WORDS_PER_PASS + u * P
                        nc.tensor.transpose(
                            own_bank[:, i, u, :], row_words[:, first_word : first_word + P], ident[:]
                        )
                nc.scalar.copy(
                    out=grouped_words[:, first_pass : first_pass + PASSES_PER_BANK],
                    in_=own_bank[:].rearrange("p g u r -> p g r u"),
                )
            x_codes[m, OWN] = own_codes[:, m]
            x_scales[m, OWN] = own_scales[:, m]
            nc.vector.quantize_mx(
                out=x_codes[m, OWN].rearrange("p g r -> p (g r)").bitcast(FP8X4),
                scales=x_scales[m, OWN].rearrange("p g r -> p (g r)"),
                in_=own_grouped[:],
            )

        def prepare_agg(m, g):
            if g == 0:
                agg_codes = agg_mx_pool.tile([P, PASSES, P], U32, align_bytes=64)
                agg_scales = agg_mx_pool.tile([P, PASSES, P], U8, align_bytes=64)
                x_codes[m, AGG] = agg_codes[:]
                x_scales[m, AGG] = agg_scales[:]
            agg_bank = banks.tile([P, PACK, P], F32, tag="bank")
            for q in range(NEIGHBOURS):
                nodes = slice(q * NODES_PER_ROWS, (q + 1) * NODES_PER_ROWS)
                for t in range(PACK):
                    first_d = g * K_PASS + t * P
                    nc.tensor.matmul(
                        out=agg_bank[:, t, nodes],
                        lhsT=neigh_rows[m][:, q, first_d : first_d + P],
                        rhs=mean_cols[:],
                        start=True,
                        stop=True,
                    )
            agg_grouped = agg_grouped_pool.tile([P, P, PACK], BF16, align_bytes=64)
            nc.scalar.copy(out=agg_grouped[:], in_=agg_bank[:].rearrange("p t r -> p r t"))
            nc.vector.quantize_mx(
                out=x_codes[m, AGG][:, g, :].bitcast(FP8X4),
                scales=x_scales[m, AGG][:, g, :],
                in_=agg_grouped[:].rearrange("p r t -> p (r t)"),
            )

        def multiply(m, product, g):
            if g == 0:
                acc[m, product] = [
                    banks.tile([P, N_TILE], F32, name="acc", tag="bank") for half in range(HALVES)
                ]
            c = PASSES * product + g
            for half in range(HALVES):
                cols = slice(half * N_TILE, (half + 1) * N_TILE)
                nc.tensor.matmul_mx(
                    out=acc[m, product][half][:],
                    lhsT=x_codes[m, product][:, g, :].bitcast(FP8X4),
                    lhsT_scale=x_scales[m, product][:, g, :],
                    rhs=w_codes[:, c, cols].bitcast(FP8X4),
                    rhs_scale=w_scales[:, c, cols],
                    start=(g == 0),
                    stop=(g == PASSES - 1),
                )

        def set_aside(m):
            nc.vector.tensor_copy(out=result[:, m, 0:N_TILE], in_=acc[m, OWN][0][:])
            nc.scalar.copy(out=result[:, m, N_TILE:H], in_=acc[m, OWN][1][:])

        def finish(m):
            for half in range(HALVES):
                cols = slice(half * N_TILE, (half + 1) * N_TILE)
                nc.vector.tensor_add(
                    out=result[:, m, cols], in0=acc[m, AGG][half][:], in1=result[:, m, cols]
                )
            nc.vector.tensor_scalar_max(out=result[:, m, :], in0=result[:, m, :], scalar1=0.0)

        for first_tile in range(0, TILES, NEIGHBOURS):
            load_own_rows(first_tile)
        for m in range(TILES):
            prepare_own(m)

        for c in range(W_ROW_BUFFERS):
            load_weight_chunk(c)
        regroup_weight_chunk(0)
        for g in range(PASSES):
            quantise_weight_chunk(PASSES * OWN + g)
            for m in range(FIRST):
                multiply(m, OWN, g)
        for m in range(FIRST):
            set_aside(m)
        for g in range(PASSES):
            quantise_weight_chunk(PASSES * AGG + g)
        for m in range(FIRST, TILES):
            for g in range(PASSES):
                multiply(m, OWN, g)
            set_aside(m)

        for m in range(ROW_BUFFERS):
            load_neigh_rows(m)
        for m in range(TILES):
            for g in range(PASSES):
                prepare_agg(m, g)
            if m + ROW_BUFFERS < TILES:
                load_neigh_rows(m + ROW_BUFFERS)
            if m > 0:
                finish(m - 1)
            for g in range(PASSES):
                multiply(m, AGG, g)
        finish(TILES - 1)

        for m in range(TILES):
            nc.sync.dma_start(out=out_view[m], in_=result[:, m, :])
